import numpy as np
import ml_dtypes


def mxq(x, axis, fmt="e4m3"):
    dtype, down = {"e4m3": (ml_dtypes.float8_e4m3fn, 7), "e5m2": (ml_dtypes.float8_e5m2, 14)}[fmt]
    v = np.moveaxis(np.asarray(x, np.float32).astype(ml_dtypes.bfloat16).astype(np.float64), axis, -1)
    blocks = v.reshape(v.shape[:-1] + (-1, 32))
    amax = np.abs(blocks).max(-1, keepdims=True)
    byte = np.maximum(np.where(amax > 0, np.frexp(amax)[1] - 1 + 127, 0) - down, 1)
    scale = np.exp2(byte - 127.0)
    codes = (blocks / scale).astype(np.float32).astype(dtype).astype(np.float64)
    return np.moveaxis((codes * scale).reshape(v.shape), -1, axis)


WIDE = False


def mx_kscale(k):
    if not WIDE:
        return np.ones(k)
    levels = np.array([10, -10, 5, -5, 0])
    a = np.random.permutation(np.resize(levels, k // 512 * 4)).reshape(k // 512, 4)
    idx = np.arange(k)
    return np.exp2(a[idx // 512, idx % 128 // 32])


BF16 = ml_dtypes.bfloat16


def bf(x):
    return np.asarray(x, np.float32).astype(BF16)


def f64(x):
    return np.asarray(x).astype(np.float64)


E2M1 = np.array([0.0, 0.5, 1.0, 1.5, 2.0, 3.0, 4.0, 6.0, -0.0, -0.5, -1.0, -1.5, -2.0, -3.0, -4.0, -6.0])


def pack_weight(w, fmt):
    k, n = w.shape
    w = f64(bf(w)).reshape(k // 32, 32, n)
    amax = np.abs(w).max(1)
    if fmt == "e4m3":
        byte = np.frexp(amax)[1] - 1 + 127 - 7
    else:
        mant, ex = np.frexp(amax / 6.0)
        byte = np.where(mant > 0.5, ex, ex - 1) + 127
    byte = np.clip(np.where(amax > 0, byte, 1), 1, 254)
    scaled = (w * np.exp2(127.0 - byte)[:, None, :]).reshape(k, n).astype(np.float32)
    by_word = np.ascontiguousarray(scaled.reshape(k // 512, 128, 4, n).transpose(0, 1, 3, 2))
    if fmt == "e4m3":
        words = by_word.astype(ml_dtypes.float8_e4m3fn).view(np.uint8)
    else:
        c = by_word.astype(ml_dtypes.float4_e2m1fn).view(np.uint8) & 0xF
        words = c[..., 0::2] | (c[..., 1::2] << 4)
    return np.ascontiguousarray(words), np.ascontiguousarray(byte.astype(np.uint8).reshape(k // 512, 16, n))


def unpack_weight(words, scales, fmt):
    g, p, n, _ = words.shape
    if fmt == "e4m3":
        vals = np.ascontiguousarray(words).view(ml_dtypes.float8_e4m3fn).astype(np.float64)
    else:
        nib = np.empty((g, p, n, 4), np.uint8)
        nib[..., 0::2] = words & 0xF
        nib[..., 1::2] = words >> 4
        vals = E2M1[nib]
    vals = vals * np.repeat(np.exp2(scales.astype(np.float64) - 127.0), 8, axis=1)[..., None]
    return vals.transpose(0, 1, 3, 2).reshape(g * 512, n)


B, S, E, H, F = 1, 512, 1024, 16, 4096
D = E // H


def setup_inputs():
    t = mx_kscale(E)
    q = bf(np.random.standard_normal((B, S, E)) * 0.7)
    k = bf(np.random.standard_normal((B, S, E)) * 0.7)
    v = bf(np.random.standard_normal((B, S, E)) * 0.7 * t)
    x = bf(np.random.standard_normal((B, S, E)))
    w_proj_words, w_proj_scales = pack_weight(np.random.standard_normal((E, E)) * 2.0 / np.sqrt(E) / t[:, None], "e4m3")
    b_proj = bf(np.random.standard_normal(E) * 0.1)
    return {
        "q": q,
        "k": k,
        "v": v,
        "x": x,
        "w_proj_words": w_proj_words,
        "w_proj_scales": w_proj_scales,
        "b_proj": b_proj,
    }


def reference(q, k, v, x, w_proj_words, w_proj_scales, b_proj):
    scores = f64(q) @ f64(k).transpose(0, 2, 1) / np.sqrt(D)
    e = np.exp(scores - scores.max(-1, keepdims=True))
    attn = (mxq(e, 2, "e4m3") @ mxq(f64(v), 1, "e4m3")) / e.sum(-1, keepdims=True)
    a = (mxq(attn, 2, "e4m3") @ unpack_weight(w_proj_words, w_proj_scales, "e4m3")) + f64(b_proj)
    return f64(x) + a

@@ -1,0 +1,314 @@
+import math
+from contextlib import ExitStack
+
+import concourse.mybir as mybir
+from concourse.masks import make_identity
+
+BF16 = mybir.dt.bfloat16
+F32 = mybir.dt.float32
+I32 = mybir.dt.int32
+U32 = mybir.dt.uint32
+U8 = mybir.dt.uint8
+FP8X4 = mybir.dt.float8_e4m3fn_x4
+ALU = mybir.AluOpType
+ACT = mybir.ActivationFunctionType
+
+P = 128
+PACK = 4
+K_PASS = P * PACK
+BANK = 512
+PSUM_BANKS = 8
+
+S = 512
+E = 1024
+HEAD = 64
+SCALE = 1.0 / math.sqrt(HEAD)
+
+ROW_TILES = S // P
+PAIR = 2
+WORD_CHUNKS = E // (PAIR * P)
+GROUPS = E // K_PASS
+OUT_CHUNKS = E // BANK
+
+FLOPS = 2 * S * S * E + 2 * S * S * E + 2 * S * E * E
+
+LAG_RECIPROCAL = 1
+LAG_TRANSPOSE_E = 2
+LAG_ATTEND = 3
+LAG_PROJECT = 4
+
+
+def tile_transformerblock_pa_kernel(tc, q, k, v, x, w_proj_words, w_proj_scales, b_proj, out):
+    nc = tc.nc
+    q_rows = q.flatten_outer_dims()
+    k_rows = k.flatten_outer_dims()
+    v_rows = v.flatten_outer_dims()
+    x_rows = x.flatten_outer_dims()
+    out_rows = out.flatten_outer_dims()
+
+    with ExitStack() as ctx:
+        sbuf = ctx.enter_context(tc.tile_pool(name="sbuf", bufs=1))
+        psum = ctx.enter_context(tc.psum_pool(name="psum", bufs=PSUM_BANKS))
+        ctx.enter_context(tc.manual_schedule())
+
+        def bank(shape, dtype, name):
+            return psum.tile(shape, dtype, name=name, tag="bank")
+
+        bias_row = sbuf.tile([P, E], BF16, name="bias_row")
+        nc.vector.memset(bias_row[:], 0.0)
+        nc.scalar.dma_start(out=bias_row[0:1, :], in_=b_proj.unsqueeze(0))
+        ones = sbuf.tile([P, P], BF16, name="ones")
+        nc.vector.memset(ones[:], 1.0)
+        w_scales = sbuf.tile([P, GROUPS, E], U8, name="w_scales", align_bytes=64)
+        nc.vector.memset(w_scales[:].bitcast(I32), 0)
+        warm_in = sbuf.tile([P, 1], F32, name="warm_in")
+        warm_out = sbuf.tile([P, 1], F32, name="warm_out")
+        nc.vector.memset(warm_in[:], 0.0)
+        nc.scalar.activation(out=warm_out[:], in_=warm_in[:], func=ACT.Exp)
+        ident_f32 = sbuf.tile([P, P], F32, name="ident_f32")
+        make_identity(nc, ident_f32[:])
+        ident_bf16 = sbuf.tile([P, P], BF16, name="ident_bf16")
+        make_identity(nc, ident_bf16[:])
+
+        q_sb = {}
+        k_sb = {}
+        x_sb = {}
+        for i in range(ROW_TILES):
+            q_sb[i] = sbuf.tile([P, E], BF16, name="q_sb%d" % i)
+            k_sb[i] = sbuf.tile([P, E], BF16, name="k_sb%d" % i)
+            x_sb[i] = sbuf.tile([P, E], BF16, name="x_sb%d" % i)
+
+        def load_rows(tile, rows, i):
+            nc.sync.dma_start(out=tile[:], in_=rows[i * P : (i + 1) * P, :])
+
+        v_raw = sbuf.tile([P, PACK, E], BF16, name="v_raw")
+        w_words = sbuf.tile([P, GROUPS, E], U32, name="w_words", align_bytes=64)
+
+        load_rows(k_sb[0], k_rows, 0)
+        load_rows(q_sb[0], q_rows, 0)
+        for j in range(1, ROW_TILES):
+            load_rows(k_sb[j], k_rows, j)
+        load_rows(q_sb[1], q_rows, 1)
+        load_rows(q_sb[2], q_rows, 2)
+        for g in range(GROUPS):
+            cols = slice(g * K_PASS, (g + 1) * K_PASS)
+            nc.sync.dma_start(out=v_raw[:, :, cols], in_=v_rows[:, cols].rearrange("(p j) f -> p j f", j=PACK))
+        load_rows(q_sb[3], q_rows, 3)
+        for g in range(GROUPS):
+            nc.sync.dma_start(
+                out=w_words[:, g, :].bitcast(I32),
+                in_=w_proj_words[g].rearrange("p n t -> p (n t)").bitcast(I32),
+            )
+        scale_rows = w_proj_scales.bitcast(I32)
+        for r in range(PACK):
+            nc.sync.dma_start(
+                out=w_scales[r : P : 32, :, :].bitcast(I32),
+                in_=scale_rows[:, r : 16 : PACK, :].rearrange("g b n -> b g n"),
+            )
+        for i in range(ROW_TILES):
+            load_rows(x_sb[i], x_rows, i)
+
+        kT_words = sbuf.tile([P, WORD_CHUNKS, S], F32, name="kT_words")
+        qT_words = {}
+        for i in range(ROW_TILES):
+            qT_words[i] = sbuf.tile([P, WORD_CHUNKS, P], F32, name="qT_words%d" % i)
+
+        def transpose_word_chunk(flipped, rows, w):
+            nc.tensor.transpose(flipped[:, w, :], rows[:].bitcast(F32)[:, w * P : (w + 1) * P], ident_f32[:])
+
+        def pairs(words):
+            return words[:].bitcast(BF16).rearrange("p w (r e) -> p w r e", e=PAIR)
+
+        def transpose_keys(j, copy):
+            flipped = bank([P, WORD_CHUNKS, P], F32, "flipped")
+            for w in range(WORD_CHUNKS):
+                transpose_word_chunk(flipped, k_sb[j], w)
+            copy(out=kT_words[:, :, j * P : (j + 1) * P], in_=flipped[:])
+
+        def transpose_first_queries():
+            flipped = bank([P, WORD_CHUNKS, P], F32, "flipped")
+            for w in range(WORD_CHUNKS):
+                transpose_word_chunk(flipped, q_sb[0], w)
+            nc.scalar.copy(out=qT_words[0][:], in_=flipped[:])
+
+        bias_all = sbuf.tile([P, E], F32, name="bias_all")
+        x_plus_b = {}
+
+        def spread_bias():
+            for n in range(OUT_CHUNKS):
+                cols = slice(n * BANK, (n + 1) * BANK)
+                b_ps = bank([P, BANK], F32, "b_ps")
+                nc.tensor.matmul(b_ps[:], lhsT=ones[:], rhs=bias_row[:, cols], start=True, stop=True)
+                nc.scalar.copy(out=bias_all[:, cols], in_=b_ps[:])
+
+        def add_bias_to_residual(i):
+            x_plus_b[i] = sbuf.tile([P, E], F32, name="x_plus_b%d" % i)
+            nc.gpsimd.tensor_tensor(out=x_plus_b[i][:], in0=x_sb[i][:], in1=bias_all[:], op=ALU.add)
+
+        v_grouped = sbuf.tile([P, E, PACK], BF16, name="v_grouped", align_bytes=64)
+        v_codes = sbuf.tile([P, E], U32, name="v_codes", align_bytes=64)
+        v_scales = sbuf.tile([P, E], U8, name="v_scales", align_bytes=64)
+
+        def regroup_v(g):
+            cols = slice(g * K_PASS, (g + 1) * K_PASS)
+            nc.vector.tensor_copy(
+                out=v_grouped[:, cols, :].rearrange("p (t c) j -> p t c j", t=PACK),
+                in_=v_raw[:, :, cols].rearrange("p j (c t) -> p t c j", t=PACK),
+            )
+
+        def quantise_v(g):
+            cols = slice(g * K_PASS, (g + 1) * K_PASS)
+            nc.vector.quantize_mx(
+                out=v_codes[:, cols].bitcast(FP8X4),
+                scales=v_scales[:, cols],
+                in_=v_grouped[:, cols, :].rearrange("p c j -> p (c j)"),
+            )
+
+        s_ps = {}
+        e_sb = {}
+        row_sum = {}
+        recip_rows = {}
+        recip_all = {}
+        e_codes = {}
+        e_scales = {}
+        a_codes = {}
+        a_scales = {}
+
+        def scores(i):
+            s_ps[i] = bank([P, S], F32, "s_ps")
+            more = i + 1 < ROW_TILES
+            if more:
+                flipped = bank([P, WORD_CHUNKS, P], F32, "flipped")
+            for w in range(WORD_CHUNKS):
+                for e in range(PAIR):
+                    nc.tensor.matmul(
+                        s_ps[i][:],
+                        lhsT=pairs(qT_words[i])[:, w, :, e],
+                        rhs=pairs(kT_words)[:, w, :, e],
+                        start=(w == 0 and e == 0),
+                        stop=(w == WORD_CHUNKS - 1 and e == PAIR - 1),
+                    )
+                if more:
+                    transpose_word_chunk(flipped, q_sb[i + 1], w)
+            if more:
+                nc.scalar.copy(out=qT_words[i + 1][:], in_=flipped[:])
+
+        def exponentials(i):
+            row_max = sbuf.tile([P, 1], F32, name="row_max%d" % i)
+            nc.vector.reduce_max(out=row_max[:], in_=s_ps[i][:], axis=mybir.AxisListType.X)
+            shift = sbuf.tile([P, 1], F32, name="shift%d" % i)
+            nc.vector.tensor_scalar(out=shift[:], in0=row_max[:], scalar1=-SCALE, scalar2=None, op0=ALU.mult)
+            e_sb[i] = sbuf.tile([P, PACK, P], BF16, name="e_sb%d" % i)
+            row_sum[i] = sbuf.tile([P, 1], F32, name="row_sum%d" % i)
+            nc.scalar.activation(
+                out=e_sb[i][:],
+                in_=s_ps[i][:].rearrange("p (c j) -> p j c", j=PACK),
+                func=ACT.Exp,
+                bias=shift[:],
+                scale=SCALE,
+                accum_out=row_sum[i][:],
+            )
+
+        def reciprocal(i):
+            recip = sbuf.tile([P, 1], F32, name="recip%d" % i)
+            nc.vector.reciprocal(out=recip[:], in_=row_sum[i][:])
+            recip_rows[i] = sbuf.tile([P, P], F32, name="recip_rows%d" % i)
+            nc.scalar.copy(out=recip_rows[i][:], in_=recip[:].to_broadcast([P, P]))
+
+        def spread_reciprocal(i):
+            r_ps = bank([P, P], F32, "r_ps")
+            nc.tensor.transpose(r_ps[:], recip_rows[i][:], ident_f32[:])
+            recip_all[i] = sbuf.tile([P, P], F32, name="recip_all%d" % i)
+            nc.scalar.copy(out=recip_all[i][:], in_=r_ps[:])
+
+        def transpose_e(i):
+            eT_ps = bank([P, PACK, P], BF16, "eT_ps")
+            for j in range(PACK):
+                nc.tensor.transpose(eT_ps[:, j, :], e_sb[i][:, j, :], ident_bf16[:])
+            e_grouped = sbuf.tile([P, P, PACK], BF16, name="e_grouped%d" % i, align_bytes=64)
+            nc.scalar.copy(out=e_grouped[:], in_=eT_ps[:].rearrange("p j r -> p r j"))
+            e_codes[i] = sbuf.tile([P, P], U32, name="e_codes%d" % i, align_bytes=64)
+            e_scales[i] = sbuf.tile([P, P], U8, name="e_scales%d" % i, align_bytes=64)
+            nc.vector.quantize_mx(
+                out=e_codes[i][:].bitcast(FP8X4),
+                scales=e_scales[i][:],
+                in_=e_grouped[:].rearrange("p r j -> p (r j)"),
+            )
+
+        def attend(i):
+            a_grouped = sbuf.tile([P, GROUPS, P, PACK], BF16, name="a_grouped%d" % i, align_bytes=64)
+            for g in range(GROUPS):
+                av_ps = bank([P, PACK, P], F32, "av_ps")
+                for t in range(PACK):
+                    cols = slice((g * PACK + t) * P, (g * PACK + t + 1) * P)
+                    nc.tensor.matmul_mx(
+                        out=av_ps[:, t, :],
+                        lhsT=v_codes[:, cols].bitcast(FP8X4),
+                        lhsT_scale=v_scales[:, cols],
+                        rhs=e_codes[i][:].bitcast(FP8X4),
+                        rhs_scale=e_scales[i][:],
+                        start=True,
+                        stop=True,
+                    )
+                nc.vector.tensor_tensor(
+                    out=a_grouped[:, g, :, :],
+                    in0=av_ps[:].rearrange("p t r -> p r t"),
+                    in1=recip_all[i][:].unsqueeze(2).to_broadcast([P, P, PACK]),
+                    op=ALU.mult,
+                )
+            a_codes[i] = sbuf.tile([P, GROUPS * P], U32, name="a_codes%d" % i, align_bytes=64)
+            a_scales[i] = sbuf.tile([P, GROUPS * P], U8, name="a_scales%d" % i, align_bytes=64)
+            nc.vector.quantize_mx(
+                out=a_codes[i][:].bitcast(FP8X4),
+                scales=a_scales[i][:],
+                in_=a_grouped[:].rearrange("p g r t -> p (g r t)"),
+            )
+
+        def project(i):
+            o_sb = sbuf.tile([P, E], F32, name="o_sb%d" % i)
+            for n in range(OUT_CHUNKS):
+                cols = slice(n * BANK, (n + 1) * BANK)
+                o_ps = bank([P, BANK], F32, "o_ps")
+                for g in range(GROUPS):
+                    rows = slice(g * P, (g + 1) * P)
+                    nc.tensor.matmul_mx(
+                        out=o_ps[:],
+                        lhsT=a_codes[i][:, rows].bitcast(FP8X4),
+                        lhsT_scale=a_scales[i][:, rows],
+                        rhs=w_words[:, g, cols].bitcast(FP8X4),
+                        rhs_scale=w_scales[:, g, cols],
+                        start=(g == 0),
+                        stop=(g == GROUPS - 1),
+                    )
+                nc.vector.tensor_tensor(out=o_sb[:, cols], in0=o_ps[:], in1=x_plus_b[i][:, cols], op=ALU.add)
+                nc.sync.dma_start(out=out_rows[i * P : (i + 1) * P, cols], in_=o_sb[:, cols])
+
+        transpose_keys(0, nc.vector.tensor_copy)
+        transpose_first_queries()
+        spread_bias()
+        for j in range(1, ROW_TILES):
+            transpose_keys(j, nc.vector.tensor_copy if j % 2 == 0 else nc.scalar.copy)
+
+        def live(i):
+            return 0 <= i < ROW_TILES
+
+        for step in range(ROW_TILES + LAG_PROJECT):
+            if live(step - LAG_ATTEND):
+                spread_reciprocal(step - LAG_ATTEND)
+            if live(step - LAG_TRANSPOSE_E):
+                transpose_e(step - LAG_TRANSPOSE_E)
+            if live(step - LAG_ATTEND):
+                attend(step - LAG_ATTEND)
+            if live(step - LAG_PROJECT):
+                project(step - LAG_PROJECT)
+            if live(step):
+                scores(step)
+                if step < GROUPS:
+                    regroup_v(step)
+                exponentials(step)
+                add_bias_to_residual(step)
+            if step == GROUPS - 1:
+                for g in range(GROUPS):
+                    quantise_v(g)
+            if live(step - LAG_RECIPROCAL):
+                reciprocal(step - LAG_RECIPROCAL)

@@ -32,10 +32,9 @@ OUT_CHUNKS = E // BANK
 
 FLOPS = 2 * S * S * E + 2 * S * S * E + 2 * S * E * E
 
-LAG_RECIPROCAL = 1
-LAG_TRANSPOSE_E = 2
-LAG_ATTEND = 3
-LAG_PROJECT = 4
+LAG_TRANSPOSE_E = 1
+LAG_ATTEND = 2
+LAG_PROJECT = 3
 
 
 def tile_transformerblock_pa_kernel(tc, q, k, v, x, w_proj_words, w_proj_scales, b_proj, out):
@@ -89,11 +88,13 @@ def tile_transformerblock_pa_kernel(tc, q, k, v, x, w_proj_words, w_proj_scales,
         for j in range(1, ROW_TILES):
             load_rows(k_sb[j], k_rows, j)
         load_rows(q_sb[1], q_rows, 1)
-        load_rows(q_sb[2], q_rows, 2)
         for g in range(GROUPS):
             cols = slice(g * K_PASS, (g + 1) * K_PASS)
             nc.sync.dma_start(out=v_raw[:, :, cols], in_=v_rows[:, cols].rearrange("(p j) f -> p j f", j=PACK))
+        load_rows(q_sb[2], q_rows, 2)
         load_rows(q_sb[3], q_rows, 3)
+        for i in range(ROW_TILES):
+            load_rows(x_sb[i], x_rows, i)
         for g in range(GROUPS):
             nc.sync.dma_start(
                 out=w_words[:, g, :].bitcast(I32),
@@ -105,8 +106,6 @@ def tile_transformerblock_pa_kernel(tc, q, k, v, x, w_proj_words, w_proj_scales,
                 out=w_scales[r : P : 32, :, :].bitcast(I32),
                 in_=scale_rows[:, r : 16 : PACK, :].rearrange("g b n -> b g n"),
             )
-        for i in range(ROW_TILES):
-            load_rows(x_sb[i], x_rows, i)
 
         kT_words = sbuf.tile([P, WORD_CHUNKS, S], F32, name="kT_words")
         qT_words = {}
@@ -125,11 +124,11 @@ def tile_transformerblock_pa_kernel(tc, q, k, v, x, w_proj_words, w_proj_scales,
                 transpose_word_chunk(flipped, k_sb[j], w)
             copy(out=kT_words[:, :, j * P : (j + 1) * P], in_=flipped[:])
 
-        def transpose_first_queries():
+        def transpose_queries(i):
             flipped = bank([P, WORD_CHUNKS, P], F32, "flipped")
             for w in range(WORD_CHUNKS):
-                transpose_word_chunk(flipped, q_sb[0], w)
-            nc.scalar.copy(out=qT_words[0][:], in_=flipped[:])
+                transpose_word_chunk(flipped, q_sb[i], w)
+            nc.scalar.copy(out=qT_words[i][:], in_=flipped[:])
 
         bias_all = sbuf.tile([P, E], F32, name="bias_all")
         x_plus_b = {}
@@ -169,28 +168,32 @@ def tile_transformerblock_pa_kernel(tc, q, k, v, x, w_proj_words, w_proj_scales,
         row_sum = {}
         recip_rows = {}
         recip_all = {}
+        e_grouped = {}
         e_codes = {}
         e_scales = {}
+        av_ps = {}
         a_codes = {}
         a_scales = {}
+        o_ps = {}
 
         def scores(i):
             s_ps[i] = bank([P, S], F32, "s_ps")
-            more = i + 1 < ROW_TILES
-            if more:
+            woven = 1 <= i < ROW_TILES - 1
+            if woven:
                 flipped = bank([P, WORD_CHUNKS, P], F32, "flipped")
-            for w in range(WORD_CHUNKS):
-                for e in range(PAIR):
-                    nc.tensor.matmul(
-                        s_ps[i][:],
-                        lhsT=pairs(qT_words[i])[:, w, :, e],
-                        rhs=pairs(kT_words)[:, w, :, e],
-                        start=(w == 0 and e == 0),
-                        stop=(w == WORD_CHUNKS - 1 and e == PAIR - 1),
-                    )
-                if more:
-                    transpose_word_chunk(flipped, q_sb[i + 1], w)
-            if more:
+            for m in range(WORD_CHUNKS * PAIR):
+                w = m // PAIR
+                e = m % PAIR
+                nc.tensor.matmul(
+                    s_ps[i][:],
+                    lhsT=pairs(qT_words[i])[:, w, :, e],
+                    rhs=pairs(kT_words)[:, w, :, e],
+                    start=(m == 0),
+                    stop=(m == WORD_CHUNKS * PAIR - 1),
+                )
+                if woven and m < WORD_CHUNKS:
+                    transpose_word_chunk(flipped, q_sb[i + 1], m)
+            if woven:
                 nc.scalar.copy(out=qT_words[i + 1][:], in_=flipped[:])
 
         def exponentials(i):
@@ -225,24 +228,25 @@ def tile_transformerblock_pa_kernel(tc, q, k, v, x, w_proj_words, w_proj_scales,
             eT_ps = bank([P, PACK, P], BF16, "eT_ps")
             for j in range(PACK):
                 nc.tensor.transpose(eT_ps[:, j, :], e_sb[i][:, j, :], ident_bf16[:])
-            e_grouped = sbuf.tile([P, P, PACK], BF16, name="e_grouped%d" % i, align_bytes=64)
-            nc.scalar.copy(out=e_grouped[:], in_=eT_ps[:].rearrange("p j r -> p r j"))
+            e_grouped[i] = sbuf.tile([P, P, PACK], BF16, name="e_grouped%d" % i, align_bytes=64)
+            nc.scalar.copy(out=e_grouped[i][:], in_=eT_ps[:].rearrange("p j r -> p r j"))
+
+        def quantise_e(i):
             e_codes[i] = sbuf.tile([P, P], U32, name="e_codes%d" % i, align_bytes=64)
             e_scales[i] = sbuf.tile([P, P], U8, name="e_scales%d" % i, align_bytes=64)
             nc.vector.quantize_mx(
                 out=e_codes[i][:].bitcast(FP8X4),
                 scales=e_scales[i][:],
-                in_=e_grouped[:].rearrange("p r j -> p (r j)"),
+                in_=e_grouped[i][:].rearrange("p r j -> p (r j)"),
             )
 
         def attend(i):
-            a_grouped = sbuf.tile([P, GROUPS, P, PACK], BF16, name="a_grouped%d" % i, align_bytes=64)
             for g in range(GROUPS):
-                av_ps = bank([P, PACK, P], F32, "av_ps")
+                av_ps[i, g] = bank([P, PACK, P], F32, "av_ps")
                 for t in range(PACK):
                     cols = slice((g * PACK + t) * P, (g * PACK + t + 1) * P)
                     nc.tensor.matmul_mx(
-                        out=av_ps[:, t, :],
+                        out=av_ps[i, g][:, t, :],
                         lhsT=v_codes[:, cols].bitcast(FP8X4),
                         lhsT_scale=v_scales[:, cols],
                         rhs=e_codes[i][:].bitcast(FP8X4),
@@ -250,9 +254,13 @@ def tile_transformerblock_pa_kernel(tc, q, k, v, x, w_proj_words, w_proj_scales,
                         start=True,
                         stop=True,
                     )
+
+        def normalise(i):
+            a_grouped = sbuf.tile([P, GROUPS, P, PACK], BF16, name="a_grouped%d" % i, align_bytes=64)
+            for g in range(GROUPS):
                 nc.vector.tensor_tensor(
                     out=a_grouped[:, g, :, :],
-                    in0=av_ps[:].rearrange("p t r -> p r t"),
+                    in0=av_ps[i, g][:].rearrange("p t r -> p r t"),
                     in1=recip_all[i][:].unsqueeze(2).to_broadcast([P, P, PACK]),
                     op=ALU.mult,
                 )
@@ -265,14 +273,13 @@ def tile_transformerblock_pa_kernel(tc, q, k, v, x, w_proj_words, w_proj_scales,
             )
 
         def project(i):
-            o_sb = sbuf.tile([P, E], F32, name="o_sb%d" % i)
             for n in range(OUT_CHUNKS):
                 cols = slice(n * BANK, (n + 1) * BANK)
-                o_ps = bank([P, BANK], F32, "o_ps")
+                o_ps[i, n] = bank([P, BANK], F32, "o_ps")
                 for g in range(GROUPS):
                     rows = slice(g * P, (g + 1) * P)
                     nc.tensor.matmul_mx(
-                        out=o_ps[:],
+                        out=o_ps[i, n][:],
                         lhsT=a_codes[i][:, rows].bitcast(FP8X4),
                         lhsT_scale=a_scales[i][:, rows],
                         rhs=w_words[:, g, cols].bitcast(FP8X4),
@@ -280,35 +287,40 @@ def tile_transformerblock_pa_kernel(tc, q, k, v, x, w_proj_words, w_proj_scales,
                         start=(g == 0),
                         stop=(g == GROUPS - 1),
                     )
-                nc.vector.tensor_tensor(out=o_sb[:, cols], in0=o_ps[:], in1=x_plus_b[i][:, cols], op=ALU.add)
+
+        def finish(i):
+            o_sb = sbuf.tile([P, E], F32, name="o_sb%d" % i)
+            for n in range(OUT_CHUNKS):
+                cols = slice(n * BANK, (n + 1) * BANK)
+                nc.vector.tensor_tensor(out=o_sb[:, cols], in0=o_ps[i, n][:], in1=x_plus_b[i][:, cols], op=ALU.add)
                 nc.sync.dma_start(out=out_rows[i * P : (i + 1) * P, cols], in_=o_sb[:, cols])
 
         transpose_keys(0, nc.vector.tensor_copy)
-        transpose_first_queries()
+        transpose_queries(0)
+        transpose_keys(1, nc.vector.tensor_copy)
+        transpose_keys(2, nc.scalar.copy)
+        transpose_keys(3, nc.vector.tensor_copy)
+        transpose_queries(1)
         spread_bias()
-        for j in range(1, ROW_TILES):
-            transpose_keys(j, nc.vector.tensor_copy if j % 2 == 0 else nc.scalar.copy)
+        regroup_v(0)
 
-        def live(i):
-            return 0 <= i < ROW_TILES
+        def for_tile(stage, i):
+            if 0 <= i < ROW_TILES:
+                stage(i)
 
         for step in range(ROW_TILES + LAG_PROJECT):
-            if live(step - LAG_ATTEND):
-                spread_reciprocal(step - LAG_ATTEND)
-            if live(step - LAG_TRANSPOSE_E):
-                transpose_e(step - LAG_TRANSPOSE_E)
-            if live(step - LAG_ATTEND):
-                attend(step - LAG_ATTEND)
-            if live(step - LAG_PROJECT):
-                project(step - LAG_PROJECT)
-            if live(step):
-                scores(step)
-                if step < GROUPS:
-                    regroup_v(step)
-                exponentials(step)
-                add_bias_to_residual(step)
-            if step == GROUPS - 1:
-                for g in range(GROUPS):
-                    quantise_v(g)
-            if live(step - LAG_RECIPROCAL):
-                reciprocal(step - LAG_RECIPROCAL)
+            for_tile(scores, step)
+            for_tile(transpose_e, step - LAG_TRANSPOSE_E)
+            for_tile(spread_reciprocal, step - LAG_ATTEND)
+            for_tile(attend, step - LAG_ATTEND)
+            for_tile(project, step - LAG_PROJECT)
+            for_tile(exponentials, step)
+            for_tile(reciprocal, step - 1)
+            if step == 0:
+                regroup_v(1)
+                quantise_v(0)
+                quantise_v(1)
+            for_tile(quantise_e, step - LAG_TRANSPOSE_E)
+            for_tile(normalise, step - LAG_ATTEND)
+            for_tile(finish, step - LAG_PROJECT)
+            for_tile(add_bias_to_residual, step)

@@ -66,8 +66,6 @@ def tile_transformerblock_pa_kernel(tc, q, k, v, x, w_proj_words, w_proj_scales,
         nc.scalar.activation(out=warm_out[:], in_=warm_in[:], func=ACT.Exp)
         ident_f32 = sbuf.tile([P, P], F32, name="ident_f32")
         make_identity(nc, ident_f32[:])
-        ident_bf16 = sbuf.tile([P, P], BF16, name="ident_bf16")
-        make_identity(nc, ident_bf16[:])
 
         q_sb = {}
         k_sb = {}
@@ -108,15 +106,18 @@ def tile_transformerblock_pa_kernel(tc, q, k, v, x, w_proj_words, w_proj_scales,
             )
 
         kT_words = sbuf.tile([P, WORD_CHUNKS, S], F32, name="kT_words")
-        qT_words = {}
+        qT = {}
         for i in range(ROW_TILES):
-            qT_words[i] = sbuf.tile([P, WORD_CHUNKS, P], F32, name="qT_words%d" % i)
+            qT[i] = sbuf.tile([P, WORD_CHUNKS, PAIR * P], BF16, name="qT%d" % i)
 
         def transpose_word_chunk(flipped, rows, w):
             nc.tensor.transpose(flipped[:, w, :], rows[:].bitcast(F32)[:, w * P : (w + 1) * P], ident_f32[:])
 
-        def pairs(words):
-            return words[:].bitcast(BF16).rearrange("p w (r e) -> p w r e", e=PAIR)
+        def pairs(values):
+            return values.rearrange("p w (r e) -> p w r e", e=PAIR)
+
+        def copy_queries_out(i, flipped):
+            nc.scalar.mul(out=qT[i][:], in_=flipped[:].bitcast(BF16), mul=SCALE)
 
         def transpose_keys(j, copy):
             flipped = bank([P, WORD_CHUNKS, P], F32, "flipped")
@@ -128,7 +129,7 @@ def tile_transformerblock_pa_kernel(tc, q, k, v, x, w_proj_words, w_proj_scales,
             flipped = bank([P, WORD_CHUNKS, P], F32, "flipped")
             for w in range(WORD_CHUNKS):
                 transpose_word_chunk(flipped, q_sb[i], w)
-            nc.scalar.copy(out=qT_words[i][:], in_=flipped[:])
+            copy_queries_out(i, flipped)
 
         bias_all = sbuf.tile([P, E], F32, name="bias_all")
         x_plus_b = {}
@@ -142,7 +143,9 @@ def tile_transformerblock_pa_kernel(tc, q, k, v, x, w_proj_words, w_proj_scales,
 
         def add_bias_to_residual(i):
             x_plus_b[i] = sbuf.tile([P, E], F32, name="x_plus_b%d" % i)
-            nc.gpsimd.tensor_tensor(out=x_plus_b[i][:], in0=x_sb[i][:], in1=bias_all[:], op=ALU.add)
+            for n in range(OUT_CHUNKS):
+                cols = slice(n * BANK, (n + 1) * BANK)
+                nc.gpsimd.tensor_tensor(out=x_plus_b[i][:, cols], in0=x_sb[i][:, cols], in1=bias_all[:, cols], op=ALU.add)
 
         v_grouped = sbuf.tile([P, E, PACK], BF16, name="v_grouped", align_bytes=64)
         v_codes = sbuf.tile([P, E], U32, name="v_codes", align_bytes=64)
@@ -186,29 +189,26 @@ def tile_transformerblock_pa_kernel(tc, q, k, v, x, w_proj_words, w_proj_scales,
                 e = m % PAIR
                 nc.tensor.matmul(
                     s_ps[i][:],
-                    lhsT=pairs(qT_words[i])[:, w, :, e],
-                    rhs=pairs(kT_words)[:, w, :, e],
+                    lhsT=pairs(qT[i][:])[:, w, :, e],
+                    rhs=pairs(kT_words[:].bitcast(BF16))[:, w, :, e],
                     start=(m == 0),
                     stop=(m == WORD_CHUNKS * PAIR - 1),
                 )
                 if woven and m < WORD_CHUNKS:
                     transpose_word_chunk(flipped, q_sb[i + 1], m)
             if woven:
-                nc.scalar.copy(out=qT_words[i + 1][:], in_=flipped[:])
+                copy_queries_out(i + 1, flipped)
 
         def exponentials(i):
-            row_max = sbuf.tile([P, 1], F32, name="row_max%d" % i)
-            nc.vector.reduce_max(out=row_max[:], in_=s_ps[i][:], axis=mybir.AxisListType.X)
-            shift = sbuf.tile([P, 1], F32, name="shift%d" % i)
-            nc.vector.tensor_scalar(out=shift[:], in0=row_max[:], scalar1=-SCALE, scalar2=None, op0=ALU.mult)
-            e_sb[i] = sbuf.tile([P, PACK, P], BF16, name="e_sb%d" % i)
+            minus_max = sbuf.tile([P, 1], F32, name="minus_max%d" % i)
+            nc.vector.reduce_max(out=minus_max[:], in_=s_ps[i][:], axis=mybir.AxisListType.X, negate=True)
+            e_sb[i] = sbuf.tile([P, PAIR, PAIR * P], BF16, name="e_sb%d" % i)
             row_sum[i] = sbuf.tile([P, 1], F32, name="row_sum%d" % i)
             nc.scalar.activation(
-                out=e_sb[i][:],
-                in_=s_ps[i][:].rearrange("p (c j) -> p j c", j=PACK),
+                out=e_sb[i][:].rearrange("p u (c e) -> p u c e", e=PAIR),
+                in_=s_ps[i][:].rearrange("p (c u e) -> p u c e", u=PAIR, e=PAIR),
                 func=ACT.Exp,
-                bias=shift[:],
-                scale=SCALE,
+                bias=minus_max[:],
                 accum_out=row_sum[i][:],
             )
 
@@ -225,11 +225,11 @@ def tile_transformerblock_pa_kernel(tc, q, k, v, x, w_proj_words, w_proj_scales,
             nc.scalar.copy(out=recip_all[i][:], in_=r_ps[:])
 
         def transpose_e(i):
-            eT_ps = bank([P, PACK, P], BF16, "eT_ps")
-            for j in range(PACK):
-                nc.tensor.transpose(eT_ps[:, j, :], e_sb[i][:, j, :], ident_bf16[:])
+            eT_ps = bank([P, PAIR, P], F32, "eT_ps")
+            for u in range(PAIR):
+                nc.tensor.transpose(eT_ps[:, u, :], e_sb[i][:].bitcast(F32)[:, u, :], ident_f32[:])
             e_grouped[i] = sbuf.tile([P, P, PACK], BF16, name="e_grouped%d" % i, align_bytes=64)
-            nc.scalar.copy(out=e_grouped[i][:], in_=eT_ps[:].rearrange("p j r -> p r j"))
+            nc.scalar.copy(out=e_grouped[i][:].bitcast(F32), in_=eT_ps[:].rearrange("p u r -> p r u"))
 
         def quantise_e(i):
             e_codes[i] = sbuf.tile([P, P], U32, name="e_codes%d" % i, align_bytes=64)
@@ -266,18 +266,21 @@ def tile_transformerblock_pa_kernel(tc, q, k, v, x, w_proj_words, w_proj_scales,
                 )
             a_codes[i] = sbuf.tile([P, GROUPS * P], U32, name="a_codes%d" % i, align_bytes=64)
             a_scales[i] = sbuf.tile([P, GROUPS * P], U8, name="a_scales%d" % i, align_bytes=64)
-            nc.vector.quantize_mx(
-                out=a_codes[i][:].bitcast(FP8X4),
-                scales=a_scales[i][:],
-                in_=a_grouped[:].rearrange("p g r t -> p (g r t)"),
-            )
+            for g in range(GROUPS):
+                rows = slice(g * P, (g + 1) * P)
+                nc.vector.quantize_mx(
+                    out=a_codes[i][:, rows].bitcast(FP8X4),
+                    scales=a_scales[i][:, rows],
+                    in_=a_grouped[:, g, :, :].rearrange("p r t -> p (r t)"),
+                )
 
         def project(i):
             for n in range(OUT_CHUNKS):
-                cols = slice(n * BANK, (n + 1) * BANK)
                 o_ps[i, n] = bank([P, BANK], F32, "o_ps")
-                for g in range(GROUPS):
-                    rows = slice(g * P, (g + 1) * P)
+            for g in range(GROUPS):
+                rows = slice(g * P, (g + 1) * P)
+                for n in range(OUT_CHUNKS):
+                    cols = slice(n * BANK, (n + 1) * BANK)
                     nc.tensor.matmul_mx(
                         out=o_ps[i, n][:],
                         lhsT=a_codes[i][:, rows].bitcast(FP8X4),

@@ -295,7 +295,11 @@ def tile_transformerblock_pa_kernel(tc, q, k, v, x, w_proj_words, w_proj_scales,
             o_sb = sbuf.tile([P, E], F32, name="o_sb%d" % i)
             for n in range(OUT_CHUNKS):
                 cols = slice(n * BANK, (n + 1) * BANK)
-                nc.vector.tensor_tensor(out=o_sb[:, cols], in0=o_ps[i, n][:], in1=x_plus_b[i][:, cols], op=ALU.add)
+                if n == OUT_CHUNKS - 1 and i < ROW_TILES - 1:
+                    nc.scalar.copy(out=o_sb[:, cols], in_=o_ps[i, n][:])
+                    nc.gpsimd.tensor_tensor(out=o_sb[:, cols], in0=o_sb[:, cols], in1=x_plus_b[i][:, cols], op=ALU.add)
+                else:
+                    nc.vector.tensor_tensor(out=o_sb[:, cols], in0=o_ps[i, n][:], in1=x_plus_b[i][:, cols], op=ALU.add)
                 nc.sync.dma_start(out=out_rows[i * P : (i + 1) * P, cols], in_=o_sb[:, cols])
 
         transpose_keys(0, nc.vector.tensor_copy)
@@ -305,6 +309,8 @@ def tile_transformerblock_pa_kernel(tc, q, k, v, x, w_proj_words, w_proj_scales,
         transpose_keys(3, nc.vector.tensor_copy)
         transpose_queries(1)
         spread_bias()
+        for i in range(ROW_TILES):
+            add_bias_to_residual(i)
         regroup_v(0)
 
         def for_tile(stage, i):
@@ -326,4 +332,3 @@ def tile_transformerblock_pa_kernel(tc, q, k, v, x, w_proj_words, w_proj_scales,
             for_tile(quantise_e, step - LAG_TRANSPOSE_E)
             for_tile(normalise, step - LAG_ATTEND)
             for_tile(finish, step - LAG_PROJECT)
-            for_tile(add_bias_to_residual, step)

@@ -54,8 +54,7 @@ def tile_transformerblock_pa_kernel(tc, q, k, v, x, w_proj_words, w_proj_scales,
             return psum.tile(shape, dtype, name=name, tag="bank")
 
         bias_row = sbuf.tile([P, E], BF16, name="bias_row")
-        nc.vector.memset(bias_row[:], 0.0)
-        nc.scalar.dma_start(out=bias_row[0:1, :], in_=b_proj.unsqueeze(0))
+        nc.vector.memset(bias_row[:].bitcast(I32), 0)
         ones = sbuf.tile([P, P], BF16, name="ones")
         nc.vector.memset(ones[:], 1.0)
         w_scales = sbuf.tile([P, GROUPS, E], U8, name="w_scales", align_bytes=64)
@@ -78,17 +77,20 @@ def tile_transformerblock_pa_kernel(tc, q, k, v, x, w_proj_words, w_proj_scales,
         def load_rows(tile, rows, i):
             nc.sync.dma_start(out=tile[:], in_=rows[i * P : (i + 1) * P, :])
 
-        v_raw = sbuf.tile([P, PACK, E], BF16, name="v_raw")
+        v_raw = {}
+        for g in range(GROUPS):
+            v_raw[g] = sbuf.tile([P, PACK, K_PASS], BF16, name="v_raw%d" % g)
         w_words = sbuf.tile([P, GROUPS, E], U32, name="w_words", align_bytes=64)
 
         load_rows(k_sb[0], k_rows, 0)
         load_rows(q_sb[0], q_rows, 0)
+        nc.sync.dma_start(out=bias_row[0:1, :], in_=b_proj.unsqueeze(0))
         for j in range(1, ROW_TILES):
             load_rows(k_sb[j], k_rows, j)
         load_rows(q_sb[1], q_rows, 1)
         for g in range(GROUPS):
             cols = slice(g * K_PASS, (g + 1) * K_PASS)
-            nc.sync.dma_start(out=v_raw[:, :, cols], in_=v_rows[:, cols].rearrange("(p j) f -> p j f", j=PACK))
+            nc.sync.dma_start(out=v_raw[g][:], in_=v_rows[:, cols].rearrange("(p j) f -> p j f", j=PACK))
         load_rows(q_sb[2], q_rows, 2)
         load_rows(q_sb[3], q_rows, 3)
         for i in range(ROW_TILES):
@@ -155,7 +157,7 @@ def tile_transformerblock_pa_kernel(tc, q, k, v, x, w_proj_words, w_proj_scales,
             cols = slice(g * K_PASS, (g + 1) * K_PASS)
             nc.vector.tensor_copy(
                 out=v_grouped[:, cols, :].rearrange("p (t c) j -> p t c j", t=PACK),
-                in_=v_raw[:, :, cols].rearrange("p j (c t) -> p t c j", t=PACK),
+                in_=v_raw[g][:].rearrange("p j (c t) -> p t c j", t=PACK),
             )
 
         def quantise_v(g):

@@ -47,11 +47,11 @@ def tile_transformerblock_pa_kernel(tc, q, k, v, x, w_proj_words, w_proj_scales,
 
     with ExitStack() as ctx:
         sbuf = ctx.enter_context(tc.tile_pool(name="sbuf", bufs=1))
-        psum = ctx.enter_context(tc.psum_pool(name="psum", bufs=PSUM_BANKS))
+        psum = ctx.enter_context(tc.psum_pool(name="psum", bufs=2))
         ctx.enter_context(tc.manual_schedule())
 
-        def bank(shape, dtype, name):
-            return psum.tile(shape, dtype, name=name, tag="bank")
+        def bank(shape, dtype, name, tag):
+            return psum.tile(shape, dtype, name=name, tag=tag)
 
         bias_row = sbuf.tile([P, E], BF16, name="bias_row")
         nc.vector.memset(bias_row[:].bitcast(I32), 0)
@@ -107,10 +107,10 @@ def tile_transformerblock_pa_kernel(tc, q, k, v, x, w_proj_words, w_proj_scales,
                 in_=scale_rows[:, r : 16 : PACK, :].rearrange("g b n -> b g n"),
             )
 
-        kT_words = sbuf.tile([P, WORD_CHUNKS, S], F32, name="kT_words")
-        qT = {}
+        kT = sbuf.tile([P, ROW_TILES, WORD_CHUNKS, PAIR * P], BF16, name="kT")
+        qT_words = {}
         for i in range(ROW_TILES):
-            qT[i] = sbuf.tile([P, WORD_CHUNKS, PAIR * P], BF16, name="qT%d" % i)
+            qT_words[i] = sbuf.tile([P, WORD_CHUNKS, P], F32, name="qT_words%d" % i)
 
         def transpose_word_chunk(flipped, rows, w):
             nc.tensor.transpose(flipped[:, w, :], rows[:].bitcast(F32)[:, w * P : (w + 1) * P], ident_f32[:])
@@ -119,16 +119,16 @@ def tile_transformerblock_pa_kernel(tc, q, k, v, x, w_proj_words, w_proj_scales,
             return values.rearrange("p w (r e) -> p w r e", e=PAIR)
 
         def copy_queries_out(i, flipped):
-            nc.scalar.mul(out=qT[i][:], in_=flipped[:].bitcast(BF16), mul=SCALE)
+            nc.scalar.copy(out=qT_words[i][:], in_=flipped[:])
 
-        def transpose_keys(j, copy):
-            flipped = bank([P, WORD_CHUNKS, P], F32, "flipped")
+        def transpose_keys(j, tag):
+            flipped = bank([P, WORD_CHUNKS, P], F32, "flipped", tag)
             for w in range(WORD_CHUNKS):
                 transpose_word_chunk(flipped, k_sb[j], w)
-            copy(out=kT_words[:, :, j * P : (j + 1) * P], in_=flipped[:])
+            nc.vector.tensor_scalar_mul(out=kT[:, j, :, :], in0=flipped[:].bitcast(BF16), scalar1=SCALE)
 
         def transpose_queries(i):
-            flipped = bank([P, WORD_CHUNKS, P], F32, "flipped")
+            flipped = bank([P, WORD_CHUNKS, P], F32, "flipped", "flip")
             for w in range(WORD_CHUNKS):
                 transpose_word_chunk(flipped, q_sb[i], w)
             copy_queries_out(i, flipped)
@@ -139,25 +139,30 @@ def tile_transformerblock_pa_kernel(tc, q, k, v, x, w_proj_words, w_proj_scales,
         def spread_bias():
             for n in range(OUT_CHUNKS):
                 cols = slice(n * BANK, (n + 1) * BANK)
-                b_ps = bank([P, BANK], F32, "b_ps")
+                b_ps = bank([P, BANK], F32, "b_ps", "attend")
                 nc.tensor.matmul(b_ps[:], lhsT=ones[:], rhs=bias_row[:, cols], start=True, stop=True)
                 nc.scalar.copy(out=bias_all[:, cols], in_=b_ps[:])
 
-        def add_bias_to_residual(i):
+        for i in range(ROW_TILES):
             x_plus_b[i] = sbuf.tile([P, E], F32, name="x_plus_b%d" % i)
-            for n in range(OUT_CHUNKS):
-                cols = slice(n * BANK, (n + 1) * BANK)
-                nc.gpsimd.tensor_tensor(out=x_plus_b[i][:, cols], in0=x_sb[i][:, cols], in1=bias_all[:, cols], op=ALU.add)
+
+        def add_bias_to_residual(i, engine, n):
+            cols = slice(n * BANK, (n + 1) * BANK)
+            engine.tensor_tensor(out=x_plus_b[i][:, cols], in0=x_sb[i][:, cols], in1=bias_all[:, cols], op=ALU.add)
 
         v_grouped = sbuf.tile([P, E, PACK], BF16, name="v_grouped", align_bytes=64)
         v_codes = sbuf.tile([P, E], U32, name="v_codes", align_bytes=64)
         v_scales = sbuf.tile([P, E], U8, name="v_scales", align_bytes=64)
 
-        def regroup_v(g):
-            cols = slice(g * K_PASS, (g + 1) * K_PASS)
-            nc.vector.tensor_copy(
-                out=v_grouped[:, cols, :].rearrange("p (t c) j -> p t c j", t=PACK),
-                in_=v_raw[g][:].rearrange("p j (c t) -> p t c j", t=PACK),
+        V_PIECE = K_PASS // 2
+
+        def regroup_v(piece, copy):
+            g = piece // 2
+            slots = slice(piece % 2 * 2, piece % 2 * 2 + 2)
+            cols = slice(piece * V_PIECE, (piece + 1) * V_PIECE)
+            copy(
+                out=v_grouped[:, cols, :].rearrange("p (t c) j -> p t c j", t=PACK // 2),
+                in_=v_raw[g][:].rearrange("p j (c t) -> p t c j", t=PACK)[:, slots, :, :],
             )
 
         def quantise_v(g):
@@ -181,53 +186,63 @@ def tile_transformerblock_pa_kernel(tc, q, k, v, x, w_proj_words, w_proj_scales,
         a_scales = {}
         o_ps = {}
 
-        def scores(i):
-            s_ps[i] = bank([P, S], F32, "s_ps")
+        def scores(i, rides):
+            s_ps[i] = bank([P, S], F32, "s_ps", "scores")
             woven = 1 <= i < ROW_TILES - 1
             if woven:
-                flipped = bank([P, WORD_CHUNKS, P], F32, "flipped")
+                flipped = bank([P, WORD_CHUNKS, P], F32, "flipped", "flip")
             for m in range(WORD_CHUNKS * PAIR):
                 w = m // PAIR
                 e = m % PAIR
                 nc.tensor.matmul(
-                    s_ps[i][:],
-                    lhsT=pairs(qT[i][:])[:, w, :, e],
-                    rhs=pairs(kT_words[:].bitcast(BF16))[:, w, :, e],
+                    s_ps[i][:].rearrange("p (j r) -> p j r", r=P),
+                    lhsT=pairs(qT_words[i][:].bitcast(BF16))[:, w, :, e],
+                    rhs=kT[:].rearrange("p j w (r e) -> p j w r e", e=PAIR)[:, :, w, :, e],
                     start=(m == 0),
                     stop=(m == WORD_CHUNKS * PAIR - 1),
                 )
                 if woven and m < WORD_CHUNKS:
                     transpose_word_chunk(flipped, q_sb[i + 1], m)
-            if woven:
-                copy_queries_out(i + 1, flipped)
+                if woven and m == WORD_CHUNKS - 1:
+                    copy_queries_out(i + 1, flipped)
+                if m in rides:
+                    rides[m]()
+
+        minus_maxes = {}
+
+        def row_maximum(i):
+            minus_maxes[i] = sbuf.tile([P, 1], F32, name="minus_max%d" % i)
+            nc.vector.reduce_max(out=minus_maxes[i][:], in_=s_ps[i][:], axis=mybir.AxisListType.X, negate=True)
 
         def exponentials(i):
-            minus_max = sbuf.tile([P, 1], F32, name="minus_max%d" % i)
-            nc.vector.reduce_max(out=minus_max[:], in_=s_ps[i][:], axis=mybir.AxisListType.X, negate=True)
             e_sb[i] = sbuf.tile([P, PAIR, PAIR * P], BF16, name="e_sb%d" % i)
             row_sum[i] = sbuf.tile([P, 1], F32, name="row_sum%d" % i)
             nc.scalar.activation(
                 out=e_sb[i][:].rearrange("p u (c e) -> p u c e", e=PAIR),
                 in_=s_ps[i][:].rearrange("p (c u e) -> p u c e", u=PAIR, e=PAIR),
                 func=ACT.Exp,
-                bias=minus_max[:],
+                bias=minus_maxes[i][:],
                 accum_out=row_sum[i][:],
             )
 
-        def reciprocal(i):
-            recip = sbuf.tile([P, 1], F32, name="recip%d" % i)
-            nc.vector.reciprocal(out=recip[:], in_=row_sum[i][:])
-            recip_rows[i] = sbuf.tile([P, P], F32, name="recip_rows%d" % i)
-            nc.scalar.copy(out=recip_rows[i][:], in_=recip[:].to_broadcast([P, P]))
+        recip = {}
 
-        def spread_reciprocal(i):
-            r_ps = bank([P, P], F32, "r_ps")
+        def reciprocal(i):
+            recip[i] = sbuf.tile([P, 1], F32, name="recip%d" % i)
+            nc.vector.reciprocal(out=recip[i][:], in_=row_sum[i][:])
+
+        def repeat_reciprocal(i):
+            recip_rows[i] = sbuf.tile([P, P], F32, name="recip_rows%d" % i)
+            nc.scalar.copy(out=recip_rows[i][:], in_=recip[i][:].to_broadcast([P, P]))
+
+        def spread_reciprocal(i, tag):
+            r_ps = bank([P, P], F32, "r_ps", tag)
             nc.tensor.transpose(r_ps[:], recip_rows[i][:], ident_f32[:])
             recip_all[i] = sbuf.tile([P, P], F32, name="recip_all%d" % i)
             nc.scalar.copy(out=recip_all[i][:], in_=r_ps[:])
 
         def transpose_e(i):
-            eT_ps = bank([P, PAIR, P], F32, "eT_ps")
+            eT_ps = bank([P, PAIR, P], F32, "eT_ps", "flip")
             for u in range(PAIR):
                 nc.tensor.transpose(eT_ps[:, u, :], e_sb[i][:].bitcast(F32)[:, u, :], ident_f32[:])
             e_grouped[i] = sbuf.tile([P, P, PACK], BF16, name="e_grouped%d" % i, align_bytes=64)
@@ -244,7 +259,7 @@ def tile_transformerblock_pa_kernel(tc, q, k, v, x, w_proj_words, w_proj_scales,
 
         def attend(i):
             for g in range(GROUPS):
-                av_ps[i, g] = bank([P, PACK, P], F32, "av_ps")
+                av_ps[i, g] = bank([P, PACK, P], F32, "av_ps", "attend")
                 for t in range(PACK):
                     cols = slice((g * PACK + t) * P, (g * PACK + t + 1) * P)
                     nc.tensor.matmul_mx(
@@ -257,80 +272,135 @@ def tile_transformerblock_pa_kernel(tc, q, k, v, x, w_proj_words, w_proj_scales,
                         stop=True,
                     )
 
-        def normalise(i):
-            a_grouped = sbuf.tile([P, GROUPS, P, PACK], BF16, name="a_grouped%d" % i, align_bytes=64)
+        a_grouped = {}
+
+        def normalise(i, g):
+            a_grouped[i, g] = sbuf.tile([P, P, PACK], BF16, name="a_grouped%d_%d" % (i, g), align_bytes=64)
+            nc.vector.tensor_tensor(
+                out=a_grouped[i, g][:],
+                in0=av_ps[i, g][:].rearrange("p t r -> p r t"),
+                in1=recip_all[i][:].unsqueeze(2).to_broadcast([P, P, PACK]),
+                op=ALU.mult,
+            )
+
+        def quantise_a(i):
             for g in range(GROUPS):
-                nc.vector.tensor_tensor(
-                    out=a_grouped[:, g, :, :],
-                    in0=av_ps[i, g][:].rearrange("p t r -> p r t"),
-                    in1=recip_all[i][:].unsqueeze(2).to_broadcast([P, P, PACK]),
-                    op=ALU.mult,
-                )
-            a_codes[i] = sbuf.tile([P, GROUPS * P], U32, name="a_codes%d" % i, align_bytes=64)
-            a_scales[i] = sbuf.tile([P, GROUPS * P], U8, name="a_scales%d" % i, align_bytes=64)
-            for g in range(GROUPS):
-                rows = slice(g * P, (g + 1) * P)
+                a_codes[i, g] = sbuf.tile([P, P], U32, name="a_codes%d_%d" % (i, g), align_bytes=64)
+                a_scales[i, g] = sbuf.tile([P, P], U8, name="a_scales%d_%d" % (i, g), align_bytes=64)
                 nc.vector.quantize_mx(
-                    out=a_codes[i][:, rows].bitcast(FP8X4),
-                    scales=a_scales[i][:, rows],
-                    in_=a_grouped[:, g, :, :].rearrange("p r t -> p (r t)"),
+                    out=a_codes[i, g][:].bitcast(FP8X4),
+                    scales=a_scales[i, g][:],
+                    in_=a_grouped[i, g][:].rearrange("p r t -> p (r t)"),
                 )
 
-        def project(i):
-            for n in range(OUT_CHUNKS):
-                o_ps[i, n] = bank([P, BANK], F32, "o_ps")
-            for g in range(GROUPS):
-                rows = slice(g * P, (g + 1) * P)
-                for n in range(OUT_CHUNKS):
-                    cols = slice(n * BANK, (n + 1) * BANK)
+        def project(i, tag, first, last, width):
+            for c in range(first, last, width):
+                o_ps[i, c] = bank([P, width], F32, "o_ps", tag)
+                for g in range(GROUPS):
                     nc.tensor.matmul_mx(
-                        out=o_ps[i, n][:],
-                        lhsT=a_codes[i][:, rows].bitcast(FP8X4),
-                        lhsT_scale=a_scales[i][:, rows],
-                        rhs=w_words[:, g, cols].bitcast(FP8X4),
-                        rhs_scale=w_scales[:, g, cols],
+                        out=o_ps[i, c][:],
+                        lhsT=a_codes[i, g][:].bitcast(FP8X4),
+                        lhsT_scale=a_scales[i, g][:],
+                        rhs=w_words[:, g, c : c + width].bitcast(FP8X4),
+                        rhs_scale=w_scales[:, g, c : c + width],
                         start=(g == 0),
                         stop=(g == GROUPS - 1),
                     )
 
-        def finish(i):
-            o_sb = sbuf.tile([P, E], F32, name="o_sb%d" % i)
-            for n in range(OUT_CHUNKS):
-                cols = slice(n * BANK, (n + 1) * BANK)
-                if n == OUT_CHUNKS - 1 and i < ROW_TILES - 1:
-                    nc.scalar.copy(out=o_sb[:, cols], in_=o_ps[i, n][:])
-                    nc.gpsimd.tensor_tensor(out=o_sb[:, cols], in0=o_sb[:, cols], in1=x_plus_b[i][:, cols], op=ALU.add)
-                else:
-                    nc.vector.tensor_tensor(out=o_sb[:, cols], in0=o_ps[i, n][:], in1=x_plus_b[i][:, cols], op=ALU.add)
-                nc.sync.dma_start(out=out_rows[i * P : (i + 1) * P, cols], in_=o_sb[:, cols])
+        def finish(i, c, width):
+            o_sb = sbuf.tile([P, width], F32, name="o_sb%d_%d" % (i, c))
+            cols = slice(c, c + width)
+            nc.vector.tensor_tensor(out=o_sb[:], in0=o_ps[i, c][:], in1=x_plus_b[i][:, cols], op=ALU.add)
+            nc.sync.dma_start(out=out_rows[i * P : (i + 1) * P, cols], in_=o_sb[:])
 
-        transpose_keys(0, nc.vector.tensor_copy)
+        def finish_by_two(i, c):
+            o_sb = sbuf.tile([P, BANK], F32, name="o_sb%d_%d" % (i, c))
+            cols = slice(c, c + BANK)
+            nc.scalar.copy(out=o_sb[:], in_=o_ps[i, c][:])
+            nc.gpsimd.tensor_tensor(out=o_sb[:], in0=o_sb[:], in1=x_plus_b[i][:, cols], op=ALU.add)
+            halves[i, c] = o_sb
+
+        halves = {}
+
+        def store_half(i, c):
+            nc.sync.dma_start(out=out_rows[i * P : (i + 1) * P, c : c + BANK], in_=halves[i, c][:])
+
+        V, A = nc.vector.tensor_copy, nc.scalar.copy
+        transpose_keys(0, "flip")
         transpose_queries(0)
-        transpose_keys(1, nc.vector.tensor_copy)
-        transpose_keys(2, nc.scalar.copy)
-        transpose_keys(3, nc.vector.tensor_copy)
+        transpose_keys(1, "project")
+        transpose_keys(2, "project")
+        transpose_keys(3, "flip")
         transpose_queries(1)
         spread_bias()
-        for i in range(ROW_TILES):
-            add_bias_to_residual(i)
-        regroup_v(0)
-
-        def for_tile(stage, i):
-            if 0 <= i < ROW_TILES:
-                stage(i)
-
-        for step in range(ROW_TILES + LAG_PROJECT):
-            for_tile(scores, step)
-            for_tile(transpose_e, step - LAG_TRANSPOSE_E)
-            for_tile(spread_reciprocal, step - LAG_ATTEND)
-            for_tile(attend, step - LAG_ATTEND)
-            for_tile(project, step - LAG_PROJECT)
-            for_tile(exponentials, step)
-            for_tile(reciprocal, step - 1)
-            if step == 0:
-                regroup_v(1)
-                quantise_v(0)
-                quantise_v(1)
-            for_tile(quantise_e, step - LAG_TRANSPOSE_E)
-            for_tile(normalise, step - LAG_ATTEND)
-            for_tile(finish, step - LAG_PROJECT)
+        for i in range(1, ROW_TILES):
+            for n in range(OUT_CHUNKS):
+                add_bias_to_residual(i, nc.gpsimd, n)
+        regroup_v(0, V)
+        regroup_v(1, V)
+        regroup_v(2, V)
+        regroup_v(3, A)
+        scores(0, {})
+        row_maximum(0)
+        exponentials(0)
+        quantise_v(0)
+        scores(1, {})
+        reciprocal(0)
+        repeat_reciprocal(0)
+        quantise_v(1)
+        transpose_e(0)
+        row_maximum(1)
+        exponentials(1)
+        quantise_e(0)
+        for n in range(OUT_CHUNKS):
+            add_bias_to_residual(0, nc.vector, n)
+        scores(2, {1: lambda: spread_reciprocal(0, "project"), 4: lambda: attend(0)})
+        reciprocal(1)
+        repeat_reciprocal(1)
+        transpose_e(1)
+        normalise(0, 0)
+        normalise(0, 1)
+        row_maximum(2)
+        exponentials(2)
+        quantise_e(1)
+        quantise_a(0)
+        scores(3, {1: lambda: spread_reciprocal(1, "project"), 4: lambda: attend(1)})
+        reciprocal(2)
+        repeat_reciprocal(2)
+        transpose_e(2)
+        spread_reciprocal(2, "flip")
+        normalise(1, 0)
+        normalise(1, 1)
+        row_maximum(3)
+        exponentials(3)
+        quantise_e(2)
+        project(0, "project", 0, E, BANK)
+        quantise_a(1)
+        project(1, "scores", 0, BANK, BANK)
+        attend(2)
+        finish(0, 0, BANK)
+        finish_by_two(0, BANK)
+        reciprocal(3)
+        repeat_reciprocal(3)
+        finish(1, 0, BANK)
+        store_half(0, BANK)
+        transpose_e(3)
+        spread_reciprocal(3, "flip")
+        normalise(2, 0)
+        quantise_e(3)
+        normalise(2, 1)
+        quantise_a(2)
+        project(1, "scores", BANK, E, BANK)
+        finish_by_two(1, BANK)
+        store_half(1, BANK)
+        attend(3)
+        project(2, "project", 0, E, BANK)
+        normalise(3, 0)
+        normalise(3, 1)
+        quantise_a(3)
+        project(3, "flip", 0, BANK, BANK // 2)
+        project(3, "scores", BANK, E, BANK // 2)
+        finish(2, 0, BANK)
+        finish(2, BANK, BANK)
+        for c in range(0, E, BANK // 2):
+            finish(3, c, BANK // 2)

import math
from contextlib import ExitStack

import concourse.mybir as mybir
from concourse.masks import make_identity

BF16 = mybir.dt.bfloat16
F32 = mybir.dt.float32
I32 = mybir.dt.int32
U32 = mybir.dt.uint32
U8 = mybir.dt.uint8
FP8X4 = mybir.dt.float8_e4m3fn_x4
ALU = mybir.AluOpType
ACT = mybir.ActivationFunctionType

P = 128
PACK = 4
K_PASS = P * PACK
BANK = 512
PSUM_BANKS = 8

S = 512
E = 1024
HEAD = 64
SCALE = 1.0 / math.sqrt(HEAD)

ROW_TILES = S // P
PAIR = 2
WORD_CHUNKS = E // (PAIR * P)
GROUPS = E // K_PASS
OUT_CHUNKS = E // BANK

FLOPS = 2 * S * S * E + 2 * S * S * E + 2 * S * E * E

LAG_TRANSPOSE_E = 1
LAG_ATTEND = 2
LAG_PROJECT = 3


def tile_transformerblock_pa_kernel(tc, q, k, v, x, w_proj_words, w_proj_scales, b_proj, out):
    nc = tc.nc
    q_rows = q.flatten_outer_dims()
    k_rows = k.flatten_outer_dims()
    v_rows = v.flatten_outer_dims()
    x_rows = x.flatten_outer_dims()
    out_rows = out.flatten_outer_dims()

    with ExitStack() as ctx:
        sbuf = ctx.enter_context(tc.tile_pool(name="sbuf", bufs=1))
        psum = ctx.enter_context(tc.psum_pool(name="psum", bufs=2))
        ctx.enter_context(tc.manual_schedule())

        def bank(shape, dtype, name, tag):
            return psum.tile(shape, dtype, name=name, tag=tag)

        bias_row = sbuf.tile([P, E], BF16, name="bias_row")
        nc.vector.memset(bias_row[:].bitcast(I32), 0)
        ones = sbuf.tile([P, P], BF16, name="ones")
        nc.vector.memset(ones[:], 1.0)
        w_scales = sbuf.tile([P, GROUPS, E], U8, name="w_scales", align_bytes=64)
        nc.vector.memset(w_scales[:].bitcast(I32), 0)
        warm_in = sbuf.tile([P, 1], F32, name="warm_in")
        warm_out = sbuf.tile([P, 1], F32, name="warm_out")
        nc.vector.memset(warm_in[:], 0.0)
        nc.scalar.activation(out=warm_out[:], in_=warm_in[:], func=ACT.Exp)
        ident_f32 = sbuf.tile([P, P], F32, name="ident_f32")
        make_identity(nc, ident_f32[:])

        q_sb = {}
        k_sb = {}
        x_sb = {}
        for i in range(ROW_TILES):
            q_sb[i] = sbuf.tile([P, E], BF16, name="q_sb%d" % i)
            k_sb[i] = sbuf.tile([P, E], BF16, name="k_sb%d" % i)
            x_sb[i] = sbuf.tile([P, E], BF16, name="x_sb%d" % i)

        def load_rows(tile, rows, i):
            nc.sync.dma_start(out=tile[:], in_=rows[i * P : (i + 1) * P, :])

        v_raw = {}
        for g in range(GROUPS):
            v_raw[g] = sbuf.tile([P, PACK, K_PASS], BF16, name="v_raw%d" % g)
        w_words = sbuf.tile([P, GROUPS, E], U32, name="w_words", align_bytes=64)

        load_rows(k_sb[0], k_rows, 0)
        load_rows(q_sb[0], q_rows, 0)
        nc.sync.dma_start(out=bias_row[0:1, :], in_=b_proj.unsqueeze(0))
        for j in range(1, ROW_TILES):
            load_rows(k_sb[j], k_rows, j)
        load_rows(q_sb[1], q_rows, 1)
        for g in range(GROUPS):
            cols = slice(g * K_PASS, (g + 1) * K_PASS)
            nc.sync.dma_start(out=v_raw[g][:], in_=v_rows[:, cols].rearrange("(p j) f -> p j f", j=PACK))
        load_rows(q_sb[2], q_rows, 2)
        load_rows(q_sb[3], q_rows, 3)
        for i in range(ROW_TILES):
            load_rows(x_sb[i], x_rows, i)
        for g in range(GROUPS):
            nc.sync.dma_start(
                out=w_words[:, g, :].bitcast(I32),
                in_=w_proj_words[g].rearrange("p n t -> p (n t)").bitcast(I32),
            )
        scale_rows = w_proj_scales.bitcast(I32)
        for r in range(PACK):
            nc.sync.dma_start(
                out=w_scales[r : P : 32, :, :].bitcast(I32),
                in_=scale_rows[:, r : 16 : PACK, :].rearrange("g b n -> b g n"),
            )

        kT = sbuf.tile([P, ROW_TILES, WORD_CHUNKS, PAIR * P], BF16, name="kT")
        qT_words = {}
        for i in range(ROW_TILES):
            qT_words[i] = sbuf.tile([P, WORD_CHUNKS, P], F32, name="qT_words%d" % i)

        def transpose_word_chunk(flipped, rows, w):
            nc.tensor.transpose(flipped[:, w, :], rows[:].bitcast(F32)[:, w * P : (w + 1) * P], ident_f32[:])

        def pairs(values):
            return values.rearrange("p w (r e) -> p w r e", e=PAIR)

        def copy_queries_out(i, flipped):
            nc.scalar.copy(out=qT_words[i][:], in_=flipped[:])

        def transpose_keys(j, tag):
            flipped = bank([P, WORD_CHUNKS, P], F32, "flipped", tag)
            for w in range(WORD_CHUNKS):
                transpose_word_chunk(flipped, k_sb[j], w)
            nc.vector.tensor_scalar_mul(out=kT[:, j, :, :], in0=flipped[:].bitcast(BF16), scalar1=SCALE)

        def transpose_queries(i):
            flipped = bank([P, WORD_CHUNKS, P], F32, "flipped", "flip")
            for w in range(WORD_CHUNKS):
                transpose_word_chunk(flipped, q_sb[i], w)
            copy_queries_out(i, flipped)

        bias_all = sbuf.tile([P, E], F32, name="bias_all")
        x_plus_b = {}

        def spread_bias():
            for n in range(OUT_CHUNKS):
                cols = slice(n * BANK, (n + 1) * BANK)
                b_ps = bank([P, BANK], F32, "b_ps", "attend")
                nc.tensor.matmul(b_ps[:], lhsT=ones[:], rhs=bias_row[:, cols], start=True, stop=True)
                nc.scalar.copy(out=bias_all[:, cols], in_=b_ps[:])

        for i in range(ROW_TILES):
            x_plus_b[i] = sbuf.tile([P, E], F32, name="x_plus_b%d" % i)

        def add_bias_to_residual(i, engine, n):
            cols = slice(n * BANK, (n + 1) * BANK)
            engine.tensor_tensor(out=x_plus_b[i][:, cols], in0=x_sb[i][:, cols], in1=bias_all[:, cols], op=ALU.add)

        v_grouped = sbuf.tile([P, E, PACK], BF16, name="v_grouped", align_bytes=64)
        v_codes = sbuf.tile([P, E], U32, name="v_codes", align_bytes=64)
        v_scales = sbuf.tile([P, E], U8, name="v_scales", align_bytes=64)

        V_PIECE = K_PASS // 2

        def regroup_v(piece, copy):
            g = piece // 2
            slots = slice(piece % 2 * 2, piece % 2 * 2 + 2)
            cols = slice(piece * V_PIECE, (piece + 1) * V_PIECE)
            copy(
                out=v_grouped[:, cols, :].rearrange("p (t c) j -> p t c j", t=PACK // 2),
                in_=v_raw[g][:].rearrange("p j (c t) -> p t c j", t=PACK)[:, slots, :, :],
            )

        def quantise_v(g):
            cols = slice(g * K_PASS, (g + 1) * K_PASS)
            nc.vector.quantize_mx(
                out=v_codes[:, cols].bitcast(FP8X4),
                scales=v_scales[:, cols],
                in_=v_grouped[:, cols, :].rearrange("p c j -> p (c j)"),
            )

        s_ps = {}
        e_sb = {}
        row_sum = {}
        recip_rows = {}
        recip_all = {}
        e_grouped = {}
        e_codes = {}
        e_scales = {}
        av_ps = {}
        a_codes = {}
        a_scales = {}
        o_ps = {}

        def scores(i, rides):
            s_ps[i] = bank([P, S], F32, "s_ps", "scores")
            woven = 1 <= i < ROW_TILES - 1
            if woven:
                flipped = bank([P, WORD_CHUNKS, P], F32, "flipped", "flip")
            for m in range(WORD_CHUNKS * PAIR):
                w = m // PAIR
                e = m % PAIR
                nc.tensor.matmul(
                    s_ps[i][:].rearrange("p (j r) -> p j r", r=P),
                    lhsT=pairs(qT_words[i][:].bitcast(BF16))[:, w, :, e],
                    rhs=kT[:].rearrange("p j w (r e) -> p j w r e", e=PAIR)[:, :, w, :, e],
                    start=(m == 0),
                    stop=(m == WORD_CHUNKS * PAIR - 1),
                )
                if woven and m < WORD_CHUNKS:
                    transpose_word_chunk(flipped, q_sb[i + 1], m)
                if woven and m == WORD_CHUNKS - 1:
                    copy_queries_out(i + 1, flipped)
                if m in rides:
                    rides[m]()

        minus_maxes = {}

        def row_maximum(i):
            minus_maxes[i] = sbuf.tile([P, 1], F32, name="minus_max%d" % i)
            nc.vector.reduce_max(out=minus_maxes[i][:], in_=s_ps[i][:], axis=mybir.AxisListType.X, negate=True)

        def exponentials(i):
            e_sb[i] = sbuf.tile([P, PAIR, PAIR * P], BF16, name="e_sb%d" % i)
            row_sum[i] = sbuf.tile([P, 1], F32, name="row_sum%d" % i)
            nc.scalar.activation(
                out=e_sb[i][:].rearrange("p u (c e) -> p u c e", e=PAIR),
                in_=s_ps[i][:].rearrange("p (c u e) -> p u c e", u=PAIR, e=PAIR),
                func=ACT.Exp,
                bias=minus_maxes[i][:],
                accum_out=row_sum[i][:],
            )

        recip = {}

        def reciprocal(i):
            recip[i] = sbuf.tile([P, 1], F32, name="recip%d" % i)
            nc.vector.reciprocal(out=recip[i][:], in_=row_sum[i][:])

        def repeat_reciprocal(i):
            recip_rows[i] = sbuf.tile([P, P], F32, name="recip_rows%d" % i)
            nc.scalar.copy(out=recip_rows[i][:], in_=recip[i][:].to_broadcast([P, P]))

        def spread_reciprocal(i, tag):
            r_ps = bank([P, P], F32, "r_ps", tag)
            nc.tensor.transpose(r_ps[:], recip_rows[i][:], ident_f32[:])
            recip_all[i] = sbuf.tile([P, P], F32, name="recip_all%d" % i)
            nc.scalar.copy(out=recip_all[i][:], in_=r_ps[:])

        def transpose_e(i):
            eT_ps = bank([P, PAIR, P], F32, "eT_ps", "flip")
            for u in range(PAIR):
                nc.tensor.transpose(eT_ps[:, u, :], e_sb[i][:].bitcast(F32)[:, u, :], ident_f32[:])
            e_grouped[i] = sbuf.tile([P, P, PACK], BF16, name="e_grouped%d" % i, align_bytes=64)
            nc.scalar.copy(out=e_grouped[i][:].bitcast(F32), in_=eT_ps[:].rearrange("p u r -> p r u"))

        def quantise_e(i):
            e_codes[i] = sbuf.tile([P, P], U32, name="e_codes%d" % i, align_bytes=64)
            e_scales[i] = sbuf.tile([P, P], U8, name="e_scales%d" % i, align_bytes=64)
            nc.vector.quantize_mx(
                out=e_codes[i][:].bitcast(FP8X4),
                scales=e_scales[i][:],
                in_=e_grouped[i][:].rearrange("p r j -> p (r j)"),
            )

        def attend(i):
            for g in range(GROUPS):
                av_ps[i, g] = bank([P, PACK, P], F32, "av_ps", "attend")
                for t in range(PACK):
                    cols = slice((g * PACK + t) * P, (g * PACK + t + 1) * P)
                    nc.tensor.matmul_mx(
                        out=av_ps[i, g][:, t, :],
                        lhsT=v_codes[:, cols].bitcast(FP8X4),
                        lhsT_scale=v_scales[:, cols],
                        rhs=e_codes[i][:].bitcast(FP8X4),
                        rhs_scale=e_scales[i][:],
                        start=True,
                        stop=True,
                    )

        a_grouped = {}

        def normalise(i, g):
            a_grouped[i, g] = sbuf.tile([P, P, PACK], BF16, name="a_grouped%d_%d" % (i, g), align_bytes=64)
            nc.vector.tensor_tensor(
                out=a_grouped[i, g][:],
                in0=av_ps[i, g][:].rearrange("p t r -> p r t"),
                in1=recip_all[i][:].unsqueeze(2).to_broadcast([P, P, PACK]),
                op=ALU.mult,
            )

        def quantise_a(i):
            for g in range(GROUPS):
                a_codes[i, g] = sbuf.tile([P, P], U32, name="a_codes%d_%d" % (i, g), align_bytes=64)
                a_scales[i, g] = sbuf.tile([P, P], U8, name="a_scales%d_%d" % (i, g), align_bytes=64)
                nc.vector.quantize_mx(
                    out=a_codes[i, g][:].bitcast(FP8X4),
                    scales=a_scales[i, g][:],
                    in_=a_grouped[i, g][:].rearrange("p r t -> p (r t)"),
                )

        def project(i, tag, first, last, width):
            for c in range(first, last, width):
                o_ps[i, c] = bank([P, width], F32, "o_ps", tag)
                for g in range(GROUPS):
                    nc.tensor.matmul_mx(
                        out=o_ps[i, c][:],
                        lhsT=a_codes[i, g][:].bitcast(FP8X4),
                        lhsT_scale=a_scales[i, g][:],
                        rhs=w_words[:, g, c : c + width].bitcast(FP8X4),
                        rhs_scale=w_scales[:, g, c : c + width],
                        start=(g == 0),
                        stop=(g == GROUPS - 1),
                    )

        def finish(i, c, width):
            o_sb = sbuf.tile([P, width], F32, name="o_sb%d_%d" % (i, c))
            cols = slice(c, c + width)
            nc.vector.tensor_tensor(out=o_sb[:], in0=o_ps[i, c][:], in1=x_plus_b[i][:, cols], op=ALU.add)
            nc.sync.dma_start(out=out_rows[i * P : (i + 1) * P, cols], in_=o_sb[:])

        def finish_by_two(i, c):
            o_sb = sbuf.tile([P, BANK], F32, name="o_sb%d_%d" % (i, c))
            cols = slice(c, c + BANK)
            nc.scalar.copy(out=o_sb[:], in_=o_ps[i, c][:])
            nc.gpsimd.tensor_tensor(out=o_sb[:], in0=o_sb[:], in1=x_plus_b[i][:, cols], op=ALU.add)
            halves[i, c] = o_sb

        halves = {}

        def store_half(i, c):
            nc.sync.dma_start(out=out_rows[i * P : (i + 1) * P, c : c + BANK], in_=halves[i, c][:])

        V, A = nc.vector.tensor_copy, nc.scalar.copy
        transpose_keys(0, "flip")
        transpose_queries(0)
        transpose_keys(1, "project")
        transpose_keys(2, "project")
        transpose_keys(3, "flip")
        transpose_queries(1)
        spread_bias()
        for i in range(1, ROW_TILES):
            for n in range(OUT_CHUNKS):
                add_bias_to_residual(i, nc.gpsimd, n)
        regroup_v(0, V)
        regroup_v(1, V)
        regroup_v(2, V)
        regroup_v(3, A)
        scores(0, {})
        row_maximum(0)
        exponentials(0)
        quantise_v(0)
        scores(1, {})
        reciprocal(0)
        repeat_reciprocal(0)
        quantise_v(1)
        transpose_e(0)
        row_maximum(1)
        exponentials(1)
        quantise_e(0)
        for n in range(OUT_CHUNKS):
            add_bias_to_residual(0, nc.vector, n)
        scores(2, {1: lambda: spread_reciprocal(0, "project"), 4: lambda: attend(0)})
        reciprocal(1)
        repeat_reciprocal(1)
        transpose_e(1)
        normalise(0, 0)
        normalise(0, 1)
        row_maximum(2)
        exponentials(2)
        quantise_e(1)
        quantise_a(0)
        scores(3, {1: lambda: spread_reciprocal(1, "project"), 4: lambda: attend(1)})
        reciprocal(2)
        repeat_reciprocal(2)
        transpose_e(2)
        spread_reciprocal(2, "flip")
        normalise(1, 0)
        normalise(1, 1)
        row_maximum(3)
        exponentials(3)
        quantise_e(2)
        project(0, "project", 0, E, BANK)
        quantise_a(1)
        project(1, "scores", 0, BANK, BANK)
        attend(2)
        finish(0, 0, BANK)
        finish_by_two(0, BANK)
        reciprocal(3)
        repeat_reciprocal(3)
        finish(1, 0, BANK)
        store_half(0, BANK)
        transpose_e(3)
        spread_reciprocal(3, "flip")
        normalise(2, 0)
        quantise_e(3)
        normalise(2, 1)
        quantise_a(2)
        project(1, "scores", BANK, E, BANK)
        finish_by_two(1, BANK)
        store_half(1, BANK)
        attend(3)
        project(2, "project", 0, E, BANK)
        normalise(3, 0)
        normalise(3, 1)
        quantise_a(3)
        project(3, "flip", 0, BANK, BANK // 2)
        project(3, "scores", BANK, E, BANK // 2)
        finish(2, 0, BANK)
        finish(2, BANK, BANK)
        for c in range(0, E, BANK // 2):
            finish(3, c, BANK // 2)
